import numpy as np
import ml_dtypes


def mxq(x, axis, fmt="e4m3"):
    dtype, down = {"e4m3": (ml_dtypes.float8_e4m3fn, 7), "e5m2": (ml_dtypes.float8_e5m2, 14)}[fmt]
    v = np.moveaxis(np.asarray(x, np.float32).astype(ml_dtypes.bfloat16).astype(np.float64), axis, -1)
    blocks = v.reshape(v.shape[:-1] + (-1, 32))
    amax = np.abs(blocks).max(-1, keepdims=True)
    byte = np.maximum(np.where(amax > 0, np.frexp(amax)[1] - 1 + 127, 0) - down, 1)
    scale = np.exp2(byte - 127.0)
    codes = (blocks / scale).astype(np.float32).astype(dtype).astype(np.float64)
    return np.moveaxis((codes * scale).reshape(v.shape), -1, axis)


WIDE = False


def mx_kscale(k):
    if not WIDE:
        return np.ones(k)
    levels = np.array([10, -10, 5, -5, 0])
    if k % 512:
        return np.exp2(np.random.permutation(np.resize(levels, k // 32))).repeat(32)
    a = np.empty((k // 512, 16))
    for p in range(k // 512):
        a[p, :8] = np.random.permutation(np.resize(levels, 8))
        for g in range(8):
            far = levels[np.abs(levels - a[p, g]) >= 10]
            a[p, g + 8] = far[np.random.randint(len(far))]
    return np.exp2(a.ravel()).repeat(32)


BF16 = ml_dtypes.bfloat16


def bf(x):
    return np.asarray(x, np.float32).astype(BF16)


def f64(x):
    return np.asarray(x).astype(np.float64)


B, N, D, L = 1, 1024, 512, 512
SEGS = N // L


def setup_inputs():
    s = mx_kscale(D)
    col = np.concatenate([np.full(D, np.sqrt(SEGS)), np.ones(D)])
    return {"x": bf(np.random.standard_normal((B, N, D)) * s),
            "w_kv": bf(np.random.standard_normal((D, D + D)) * col / np.sqrt(D) / s[:, None])}


def reference(x, w_kv):
    kv = mxq(f64(x), 2, "e4m3") @ mxq(f64(w_kv), 0, "e4m3")
    k, v = kv[..., :D], kv[..., D:]
    keys_lm = k.reshape(B, L, SEGS, D).mean(axis=2)
    vals_lm = v.reshape(B, L, SEGS, D).mean(axis=2)
    return v, keys_lm, vals_lm

@@ -1,0 +1,176 @@
+from contextlib import ExitStack
+
+import concourse.mybir as mybir
+from concourse.masks import make_identity
+
+F32 = mybir.dt.float32
+BF16 = mybir.dt.bfloat16
+U32 = mybir.dt.uint32
+U8 = mybir.dt.uint8
+FP8X4 = mybir.dt.float8_e4m3fn_x4
+COPY = mybir.ActivationFunctionType.Copy
+
+P = 128
+PACK = 4
+PAIR = 2
+WORDS = PACK // PAIR
+TOKENS = 1024
+D = 512
+SEG = 2
+GROUPS = TOKENS // (P * SEG)
+AHEAD = 2
+RUN = 4
+KEYS, VALUES = 0, 1
+PSUM_BANKS = 8
+XT_BANKS = 3
+WARM_MATMULS = 7
+
+FLOPS = 2 * TOKENS * D * (2 * D)
+
+
+def tile_ammattention_pa_kernel(tc, x, w_kv, out_0, out_1, out_2):
+    nc = tc.nc
+
+    x_view = x.rearrange("b (p g s) k -> (b p) g (s k)", g=GROUPS, s=SEG)
+    v_view = out_0.rearrange("b (p g s) d -> (b p) g s d", g=GROUPS, s=SEG)
+    mean_views = {
+        KEYS: out_1.rearrange("b (p g) d -> (b p) g d", g=GROUPS),
+        VALUES: out_2.rearrange("b (p g) d -> (b p) g d", g=GROUPS),
+    }
+    w_view = w_kv.rearrange("(q u e) (h c) -> q h u e c", u=WORDS, e=PAIR, h=2)
+
+    with ExitStack() as ctx:
+        const = ctx.enter_context(tc.tile_pool(name="const", bufs=1))
+        w_pool = ctx.enter_context(tc.tile_pool(name="w", bufs=2))
+        x_pool = ctx.enter_context(tc.tile_pool(name="x", bufs=GROUPS))
+        x_mx_pool = ctx.enter_context(tc.tile_pool(name="x_mx", bufs=GROUPS * SEG))
+        out_pool = ctx.enter_context(tc.tile_pool(name="out", bufs=GROUPS * SEG))
+        xt_psum = ctx.enter_context(tc.psum_pool(name="xt", bufs=XT_BANKS))
+        acc_psum = ctx.enter_context(tc.psum_pool(name="acc", bufs=PSUM_BANKS - XT_BANKS))
+        ctx.enter_context(tc.manual_schedule())
+
+        def load_w(half):
+            w_raw = w_pool.tile([P, PACK, D], BF16)
+            for u in range(WORDS):
+                nc.sync.dma_start(
+                    out=w_raw[:, u * PAIR : (u + 1) * PAIR, :], in_=w_view[:, half, u]
+                )
+            return w_raw
+
+        def load_x(g):
+            x_raw = x_pool.tile([P, SEG, D], BF16)
+            nc.sync.dma_start(
+                out=x_raw[:].rearrange("p s k -> p (s k)"), in_=x_view[:, g]
+            )
+            return x_raw
+
+        def regroup_w(w_raw, scalar_cols):
+            w_grouped = w_pool.tile([P, D, PACK], BF16, align_bytes=64)
+            cut = D - scalar_cols
+            nc.vector.tensor_copy(
+                out=w_grouped[:, :cut, :].rearrange("q (c i) t -> q c t i", i=RUN),
+                in_=w_raw[:, :, :cut].rearrange("q t (c i) -> q c t i", i=RUN),
+            )
+            if scalar_cols > 0:
+                nc.scalar.copy(
+                    out=w_grouped[:, cut:, :].rearrange("q (c i) t -> q c t i", i=RUN),
+                    in_=w_raw[:, :, cut:].rearrange("q t (c i) -> q c t i", i=RUN),
+                )
+            return w_grouped
+
+        def quantise_w(w_grouped):
+            w_codes = w_pool.tile([P, D], U32, align_bytes=64)
+            w_scales = w_pool.tile([P, D], U8, align_bytes=64)
+            nc.vector.quantize_mx(
+                out=w_codes[:].bitcast(FP8X4),
+                scales=w_scales[:],
+                in_=w_grouped[:].rearrange("q c t -> q (c t)"),
+            )
+            return w_codes, w_scales
+
+        def quantise_x(x_raw, s):
+            words = x_raw[:, s, :].bitcast(F32).rearrange("p (q u) -> p u q", u=WORDS)
+            xt = xt_psum.tile([P, WORDS, P], F32)
+            for u in range(WORDS):
+                nc.tensor.transpose(xt[:, u, :], words[:, u, :], identity[:])
+            x_grouped = x_mx_pool.tile([P, P * PACK], BF16, align_bytes=64)
+            nc.scalar.copy(
+                out=x_grouped[:].bitcast(F32).rearrange("q (p u) -> q p u", u=WORDS),
+                in_=xt[:].rearrange("q u p -> q p u"),
+            )
+            x_codes = x_mx_pool.tile([P, P], U32, align_bytes=64)
+            x_scales = x_mx_pool.tile([P, P], U8, align_bytes=64)
+            nc.vector.quantize_mx(
+                out=x_codes[:].bitcast(FP8X4), scales=x_scales[:], in_=x_grouped[:]
+            )
+            return x_codes, x_scales
+
+        def quantise_group(g):
+            return [quantise_x(x_raws[g], s) for s in range(SEG)]
+
+        def multiply(acc, x_mx, w_mx, start, stop):
+            x_codes, x_scales = x_mx
+            w_codes, w_scales = w_mx
+            nc.tensor.matmul_mx(
+                out=acc[:],
+                lhsT=x_codes[:].bitcast(FP8X4),
+                lhsT_scale=x_scales[:],
+                rhs=w_codes[:].bitcast(FP8X4),
+                rhs_scale=w_scales[:],
+                start=start,
+                stop=stop,
+            )
+
+        def store_values(g):
+            for s in range(SEG):
+                acc = acc_psum.tile([P, D], F32, tag="acc")
+                multiply(acc, x_mx[g][s], w_mx[VALUES], start=True, stop=True)
+                v_sb = out_pool.tile([P, D], F32)
+                if s % 2 == 0:
+                    nc.scalar.copy(out=v_sb[:], in_=acc[:])
+                else:
+                    nc.vector.tensor_copy(out=v_sb[:], in_=acc[:])
+                nc.sync.dma_start(out=v_view[:, g, s], in_=v_sb[:])
+
+        def store_mean(g, half):
+            acc = acc_psum.tile([P, D], F32, tag="acc")
+            for s in range(SEG):
+                multiply(acc, x_mx[g][s], w_mx[half], start=(s == 0), stop=(s == SEG - 1))
+            mean = out_pool.tile([P, D], F32, tag="mean%d" % half)
+            if (g + half) % 2 == 1:
+                nc.scalar.activation(out=mean[:], in_=acc[:], func=COPY, scale=1.0 / SEG)
+            else:
+                nc.vector.tensor_scalar_mul(out=mean[:], in0=acc[:], scalar1=1.0 / SEG)
+            nc.sync.dma_start(out=mean_views[half][:, g], in_=mean[:])
+
+        w_raw_values = load_w(VALUES)
+        x_raws = [load_x(g) for g in range(GROUPS)]
+        w_raw_keys = load_w(KEYS)
+
+        warm = const.tile([P, 1], F32)
+        nc.vector.memset(warm[:], 0.0)
+        nc.scalar.activation(out=warm[:], in_=warm[:], func=COPY, scale=1.0 / SEG)
+
+        identity = const.tile([P, P], F32)
+        make_identity(nc, identity[:])
+
+        unread = acc_psum.tile([P, P], F32, tag="acc")
+        for i in range(WARM_MATMULS):
+            nc.tensor.matmul(
+                out=unread[:], lhsT=identity[:], rhs=identity[:], start=True, stop=True
+            )
+
+        w_mx = {VALUES: quantise_w(regroup_w(w_raw_values, scalar_cols=D // 4))}
+        x_mx = [quantise_group(g) for g in range(AHEAD)]
+
+        for g in range(GROUPS):
+            store_values(g)
+            store_mean(g, VALUES)
+            if g == 0:
+                w_grouped_keys = regroup_w(w_raw_keys, scalar_cols=0)
+            if g + AHEAD < GROUPS:
+                x_mx.append(quantise_group(g + AHEAD))
+            if g + AHEAD == GROUPS:
+                w_mx[KEYS] = quantise_w(w_grouped_keys)
+        for g in range(GROUPS):
+            store_mean(g, KEYS)

@@ -18,12 +18,14 @@ TOKENS = 1024
 D = 512
 SEG = 2
 GROUPS = TOKENS // (P * SEG)
-AHEAD = 2
 RUN = 4
 KEYS, VALUES = 0, 1
 PSUM_BANKS = 8
 XT_BANKS = 3
-WARM_MATMULS = 7
+EVEN, ODD = 0, 1
+BOTH = (EVEN, ODD)
+COLUMN_HALVES = (slice(0, D // 2), slice(D // 2, D))
+VECTOR_COLS = 144
 
 FLOPS = 2 * TOKENS * D * (2 * D)
 
@@ -33,11 +35,9 @@ def tile_ammattention_pa_kernel(tc, x, w_kv, out_0, out_1, out_2):
 
     x_view = x.rearrange("b (p g s) k -> (b p) g (s k)", g=GROUPS, s=SEG)
     v_view = out_0.rearrange("b (p g s) d -> (b p) g s d", g=GROUPS, s=SEG)
-    mean_views = {
-        KEYS: out_1.rearrange("b (p g) d -> (b p) g d", g=GROUPS),
-        VALUES: out_2.rearrange("b (p g) d -> (b p) g d", g=GROUPS),
-    }
-    w_view = w_kv.rearrange("(q u e) (h c) -> q h u e c", u=WORDS, e=PAIR, h=2)
+    key_means = out_1.rearrange("b (p g) d -> (b p) g d", g=GROUPS)
+    value_means = out_2.rearrange("b (p g) d -> (b p) g d", g=GROUPS)
+    w_view = w_kv.rearrange("(q t) (h c) -> q h t c", t=PACK, h=2)
 
     with ExitStack() as ctx:
         const = ctx.enter_context(tc.tile_pool(name="const", bufs=1))
@@ -51,10 +51,7 @@ def tile_ammattention_pa_kernel(tc, x, w_kv, out_0, out_1, out_2):
 
         def load_w(half):
             w_raw = w_pool.tile([P, PACK, D], BF16)
-            for u in range(WORDS):
-                nc.sync.dma_start(
-                    out=w_raw[:, u * PAIR : (u + 1) * PAIR, :], in_=w_view[:, half, u]
-                )
+            nc.sync.dma_start(out=w_raw[:], in_=w_view[:, half])
             return w_raw
 
         def load_x(g):
@@ -64,87 +61,81 @@ def tile_ammattention_pa_kernel(tc, x, w_kv, out_0, out_1, out_2):
             )
             return x_raw
 
-        def regroup_w(w_raw, scalar_cols):
-            w_grouped = w_pool.tile([P, D, PACK], BF16, align_bytes=64)
-            cut = D - scalar_cols
-            nc.vector.tensor_copy(
-                out=w_grouped[:, :cut, :].rearrange("q (c i) t -> q c t i", i=RUN),
-                in_=w_raw[:, :, :cut].rearrange("q t (c i) -> q c t i", i=RUN),
+        def regroup(copy, w_grouped, w_raw, cols):
+            copy(
+                out=w_grouped[:, cols, :].rearrange("q (c i) t -> q c t i", i=RUN),
+                in_=w_raw[:, :, cols].rearrange("q t (c i) -> q c t i", i=RUN),
             )
-            if scalar_cols > 0:
-                nc.scalar.copy(
-                    out=w_grouped[:, cut:, :].rearrange("q (c i) t -> q c t i", i=RUN),
-                    in_=w_raw[:, :, cut:].rearrange("q t (c i) -> q c t i", i=RUN),
-                )
-            return w_grouped
 
-        def quantise_w(w_grouped):
-            w_codes = w_pool.tile([P, D], U32, align_bytes=64)
-            w_scales = w_pool.tile([P, D], U8, align_bytes=64)
+        def quantise_w(w_mx, w_grouped, cols):
+            w_codes, w_scales = w_mx
             nc.vector.quantize_mx(
-                out=w_codes[:].bitcast(FP8X4),
-                scales=w_scales[:],
-                in_=w_grouped[:].rearrange("q c t -> q (c t)"),
+                out=w_codes[:, cols].bitcast(FP8X4),
+                scales=w_scales[:, cols],
+                in_=w_grouped[:, cols, :].rearrange("q c t -> q (c t)"),
             )
-            return w_codes, w_scales
 
-        def quantise_x(x_raw, s):
-            words = x_raw[:, s, :].bitcast(F32).rearrange("p (q u) -> p u q", u=WORDS)
+        def transpose_x(g, s):
+            words = x_raws[g][:, s, :].bitcast(F32).rearrange("p (q u) -> p u q", u=WORDS)
             xt = xt_psum.tile([P, WORDS, P], F32)
             for u in range(WORDS):
                 nc.tensor.transpose(xt[:, u, :], words[:, u, :], identity[:])
-            x_grouped = x_mx_pool.tile([P, P * PACK], BF16, align_bytes=64)
-            nc.scalar.copy(
-                out=x_grouped[:].bitcast(F32).rearrange("q (p u) -> q p u", u=WORDS),
-                in_=xt[:].rearrange("q u p -> q p u"),
+            xts[g, s] = xt
+
+        def group_x(copy, g, s):
+            grouped = x_mx_pool.tile([P, P * PACK], BF16, align_bytes=64)
+            copy(
+                out=grouped[:].bitcast(F32).rearrange("q (p u) -> q p u", u=WORDS),
+                in_=xts[g, s][:].rearrange("q u p -> q p u"),
             )
+            x_grouped[g, s] = grouped
+
+        def quantise_x(g, s):
             x_codes = x_mx_pool.tile([P, P], U32, align_bytes=64)
             x_scales = x_mx_pool.tile([P, P], U8, align_bytes=64)
             nc.vector.quantize_mx(
-                out=x_codes[:].bitcast(FP8X4), scales=x_scales[:], in_=x_grouped[:]
+                out=x_codes[:].bitcast(FP8X4), scales=x_scales[:], in_=x_grouped[g, s][:]
             )
-            return x_codes, x_scales
+            x_mx[g, s] = x_codes, x_scales
 
-        def quantise_group(g):
-            return [quantise_x(x_raws[g], s) for s in range(SEG)]
-
-        def multiply(acc, x_mx, w_mx, start, stop):
-            x_codes, x_scales = x_mx
-            w_codes, w_scales = w_mx
-            nc.tensor.matmul_mx(
-                out=acc[:],
-                lhsT=x_codes[:].bitcast(FP8X4),
-                lhsT_scale=x_scales[:],
-                rhs=w_codes[:].bitcast(FP8X4),
-                rhs_scale=w_scales[:],
-                start=start,
-                stop=stop,
-            )
-
-        def store_values(g):
-            for s in range(SEG):
-                acc = acc_psum.tile([P, D], F32, tag="acc")
-                multiply(acc, x_mx[g][s], w_mx[VALUES], start=True, stop=True)
-                v_sb = out_pool.tile([P, D], F32)
-                if s % 2 == 0:
-                    nc.scalar.copy(out=v_sb[:], in_=acc[:])
-                else:
-                    nc.vector.tensor_copy(out=v_sb[:], in_=acc[:])
-                nc.sync.dma_start(out=v_view[:, g, s], in_=v_sb[:])
-
-        def store_mean(g, half):
+        def multiply(g, tokens, w_mx, cols=slice(0, D)):
             acc = acc_psum.tile([P, D], F32, tag="acc")
-            for s in range(SEG):
-                multiply(acc, x_mx[g][s], w_mx[half], start=(s == 0), stop=(s == SEG - 1))
-            mean = out_pool.tile([P, D], F32, tag="mean%d" % half)
-            if (g + half) % 2 == 1:
-                nc.scalar.activation(out=mean[:], in_=acc[:], func=COPY, scale=1.0 / SEG)
-            else:
-                nc.vector.tensor_scalar_mul(out=mean[:], in0=acc[:], scalar1=1.0 / SEG)
-            nc.sync.dma_start(out=mean_views[half][:, g], in_=mean[:])
+            w_codes, w_scales = w_mx
+            for s in tokens:
+                x_codes, x_scales = x_mx[g, s]
+                nc.tensor.matmul_mx(
+                    out=acc[:, cols],
+                    lhsT=x_codes[:].bitcast(FP8X4),
+                    lhsT_scale=x_scales[:],
+                    rhs=w_codes[:, cols].bitcast(FP8X4),
+                    rhs_scale=w_scales[:, cols],
+                    start=(s == tokens[0]),
+                    stop=(s == tokens[-1]),
+                )
+            return acc
 
+        def multiply_values(g):
+            return [multiply(g, tokens, values_mx) for tokens in ((EVEN,), BOTH, (ODD,))]
+
+        def scalar_halve(out, acc):
+            nc.scalar.activation(out=out, in_=acc[:], func=COPY, scale=1.0 / SEG)
+
+        def vector_halve(out, acc):
+            nc.vector.tensor_scalar_mul(out=out, in0=acc[:], scalar1=1.0 / SEG)
+
+        def store_mean(halve, means, g, acc):
+            mean = out_pool.tile([P, D], F32)
+            halve(mean[:], acc)
+            nc.sync.dma_start(out=means[:, g], in_=mean[:])
+
+        def store_value(copy, g, s, acc):
+            v_sb = out_pool.tile([P, D], F32)
+            copy(out=v_sb[:], in_=acc[:])
+            nc.sync.dma_start(out=v_view[:, g, s], in_=v_sb[:])
+
+        x_raws = [load_x(0)]
         w_raw_values = load_w(VALUES)
-        x_raws = [load_x(g) for g in range(GROUPS)]
+        x_raws += [load_x(g) for g in range(1, GROUPS)]
         w_raw_keys = load_w(KEYS)
 
         warm = const.tile([P, 1], F32)
@@ -155,22 +146,88 @@ def tile_ammattention_pa_kernel(tc, x, w_kv, out_0, out_1, out_2):
         make_identity(nc, identity[:])
 
         unread = acc_psum.tile([P, P], F32, tag="acc")
-        for i in range(WARM_MATMULS):
-            nc.tensor.matmul(
-                out=unread[:], lhsT=identity[:], rhs=identity[:], start=True, stop=True
+
+        def keep_busy(matmuls):
+            for i in range(matmuls):
+                nc.tensor.matmul(
+                    out=unread[:], lhsT=identity[:], rhs=identity[:], start=True, stop=True
+                )
+
+        xts, x_grouped, x_mx = {}, {}, {}
+        scalar_copy, vector_copy = nc.scalar.copy, nc.vector.tensor_copy
+        values_mx, keys_mx = [
+            (
+                w_pool.tile([P, D], U32, align_bytes=64, name="w_codes"),
+                w_pool.tile([P, D], U8, align_bytes=64, name="w_scales"),
             )
+            for half in range(2)
+        ]
+        values_grouped = w_pool.tile([P, D, PACK], BF16, align_bytes=64, name="w_grouped")
+        keys_grouped = w_pool.tile([P, D, PACK], BF16, align_bytes=64, name="w_grouped")
 
-        w_mx = {VALUES: quantise_w(regroup_w(w_raw_values, scalar_cols=D // 4))}
-        x_mx = [quantise_group(g) for g in range(AHEAD)]
+        keep_busy(4)
+        transpose_x(0, EVEN)
+        transpose_x(0, ODD)
+        group_x(vector_copy, 0, EVEN)
+        group_x(scalar_copy, 0, ODD)
+        keep_busy(2)
+        quantise_x(0, EVEN)
+
+        for cols in COLUMN_HALVES:
+            cut = cols.start + VECTOR_COLS
+            regroup(vector_copy, values_grouped, w_raw_values, slice(cols.start, cut))
+            regroup(scalar_copy, values_grouped, w_raw_values, slice(cut, cols.stop))
+        quantise_x(0, ODD)
+        for cols in COLUMN_HALVES:
+            quantise_w(values_mx, values_grouped, cols)
+
+        transpose_x(1, EVEN)
+        transpose_x(1, ODD)
+        group_x(scalar_copy, 1, EVEN)
+        group_x(vector_copy, 1, ODD)
+
+        halves = [multiply(0, (EVEN,), values_mx, cols) for cols in COLUMN_HALVES]
+        quantise_x(1, EVEN)
+        v_sb = out_pool.tile([P, D], F32)
+        for copy, cols, acc in zip((scalar_copy, vector_copy), COLUMN_HALVES, halves):
+            copy(out=v_sb[:, cols], in_=acc[:, cols])
+        nc.sync.dma_start(out=v_view[:, 0, EVEN], in_=v_sb[:])
+        odd = multiply(0, (ODD,), values_mx)
+        sums = multiply(0, BOTH, values_mx)
+        transpose_x(2, EVEN)
+        quantise_x(1, ODD)
+        store_value(vector_copy, 0, ODD, odd)
+        store_mean(scalar_halve, value_means, 0, sums)
+
+        transpose_x(2, ODD)
+        even, sums, odd = multiply_values(1)
+        group_x(vector_copy, 2, EVEN)
+        transpose_x(3, EVEN)
+        regroup(vector_copy, keys_grouped, w_raw_keys, COLUMN_HALVES[0])
+        quantise_x(2, EVEN)
+        store_value(scalar_copy, 1, EVEN, even)
+        group_x(scalar_copy, 2, ODD)
+        transpose_x(3, ODD)
+        store_mean(vector_halve, value_means, 1, sums)
+        quantise_x(2, ODD)
+        store_value(scalar_copy, 1, ODD, odd)
+
+        even, sums, odd = multiply_values(2)
+        group_x(vector_copy, 3, EVEN)
+        group_x(scalar_copy, 3, ODD)
+        quantise_x(3, EVEN)
+        quantise_x(3, ODD)
+        regroup(vector_copy, keys_grouped, w_raw_keys, COLUMN_HALVES[1])
+        store_value(scalar_copy, 2, EVEN, even)
+        quantise_w(keys_mx, keys_grouped, slice(0, D))
+        store_mean(scalar_halve, value_means, 2, sums)
+        store_value(scalar_copy, 2, ODD, odd)
+
+        even, sums, odd = multiply_values(3)
+        store_value(vector_copy, 3, EVEN, even)
+        store_mean(scalar_halve, value_means, 3, sums)
+        store_value(scalar_copy, 3, ODD, odd)
 
         for g in range(GROUPS):
-            store_values(g)
-            store_mean(g, VALUES)
-            if g == 0:
-                w_grouped_keys = regroup_w(w_raw_keys, scalar_cols=0)
-            if g + AHEAD < GROUPS:
-                x_mx.append(quantise_group(g + AHEAD))
-            if g + AHEAD == GROUPS:
-                w_mx[KEYS] = quantise_w(w_grouped_keys)
-        for g in range(GROUPS):
-            store_mean(g, KEYS)
+            halve = vector_halve if g % 2 == 0 else scalar_halve
+            store_mean(halve, key_means, g, multiply(g, BOTH, keys_mx))

@@ -9,6 +9,8 @@ U32 = mybir.dt.uint32
 U8 = mybir.dt.uint8
 FP8X4 = mybir.dt.float8_e4m3fn_x4
 COPY = mybir.ActivationFunctionType.Copy
+MULT = mybir.AluOpType.mult
+ADD = mybir.AluOpType.add
 
 P = 128
 PACK = 4
@@ -18,6 +20,7 @@ TOKENS = 1024
 D = 512
 SEG = 2
 GROUPS = TOKENS // (P * SEG)
+GPSIMD_COLS = 64
 RUN = 4
 KEYS, VALUES = 0, 1
 PSUM_BANKS = 8
@@ -33,7 +36,7 @@ FLOPS = 2 * TOKENS * D * (2 * D)
 def tile_ammattention_pa_kernel(tc, x, w_kv, out_0, out_1, out_2):
     nc = tc.nc
 
-    x_view = x.rearrange("b (p g s) k -> (b p) g (s k)", g=GROUPS, s=SEG)
+    x_view = x.rearrange("b (p g s) k -> (b p) g s k", g=GROUPS, s=SEG)
     v_view = out_0.rearrange("b (p g s) d -> (b p) g s d", g=GROUPS, s=SEG)
     key_means = out_1.rearrange("b (p g) d -> (b p) g d", g=GROUPS)
     value_means = out_2.rearrange("b (p g) d -> (b p) g d", g=GROUPS)
@@ -54,12 +57,11 @@ def tile_ammattention_pa_kernel(tc, x, w_kv, out_0, out_1, out_2):
             nc.sync.dma_start(out=w_raw[:], in_=w_view[:, half])
             return w_raw
 
-        def load_x(g):
-            x_raw = x_pool.tile([P, SEG, D], BF16)
+        def load_x(g, tokens):
             nc.sync.dma_start(
-                out=x_raw[:].rearrange("p s k -> p (s k)"), in_=x_view[:, g]
+                out=x_raws[g][:, tokens, :].rearrange("p s k -> p (s k)"),
+                in_=x_view[:, g, tokens, :].rearrange("p s k -> p (s k)"),
             )
-            return x_raw
 
         def regroup(copy, w_grouped, w_raw, cols):
             copy(
@@ -114,9 +116,6 @@ def tile_ammattention_pa_kernel(tc, x, w_kv, out_0, out_1, out_2):
                 )
             return acc
 
-        def multiply_values(g):
-            return [multiply(g, tokens, values_mx) for tokens in ((EVEN,), BOTH, (ODD,))]
-
         def scalar_halve(out, acc):
             nc.scalar.activation(out=out, in_=acc[:], func=COPY, scale=1.0 / SEG)
 
@@ -128,14 +127,17 @@ def tile_ammattention_pa_kernel(tc, x, w_kv, out_0, out_1, out_2):
             halve(mean[:], acc)
             nc.sync.dma_start(out=means[:, g], in_=mean[:])
 
-        def store_value(copy, g, s, acc):
+        def store_value(g, s, acc):
             v_sb = out_pool.tile([P, D], F32)
-            copy(out=v_sb[:], in_=acc[:])
+            nc.scalar.copy(out=v_sb[:], in_=acc[:])
             nc.sync.dma_start(out=v_view[:, g, s], in_=v_sb[:])
 
-        x_raws = [load_x(0)]
+        x_raws = [x_pool.tile([P, SEG, D], BF16, name="x_raw") for g in range(GROUPS)]
+        load_x(0, slice(EVEN, EVEN + 1))
         w_raw_values = load_w(VALUES)
-        x_raws += [load_x(g) for g in range(1, GROUPS)]
+        load_x(0, slice(ODD, ODD + 1))
+        for g in range(1, GROUPS):
+            load_x(g, slice(0, SEG))
         w_raw_keys = load_w(KEYS)
 
         warm = const.tile([P, 1], F32)
@@ -165,21 +167,33 @@ def tile_ammattention_pa_kernel(tc, x, w_kv, out_0, out_1, out_2):
         values_grouped = w_pool.tile([P, D, PACK], BF16, align_bytes=64, name="w_grouped")
         keys_grouped = w_pool.tile([P, D, PACK], BF16, align_bytes=64, name="w_grouped")
 
-        keep_busy(4)
+        for c in range(0, D, GPSIMD_COLS):
+            cols = slice(c, c + GPSIMD_COLS)
+            nc.gpsimd.tensor_scalar(
+                out=keys_grouped[:, cols, :],
+                in0=w_raw_keys[:, :, cols].rearrange("q t c -> q c t"),
+                scalar1=1.0,
+                scalar2=0.0,
+                op0=MULT,
+                op1=ADD,
+            )
+
+        keep_busy(3)
         transpose_x(0, EVEN)
-        transpose_x(0, ODD)
-        group_x(vector_copy, 0, EVEN)
-        group_x(scalar_copy, 0, ODD)
-        keep_busy(2)
+        group_x(scalar_copy, 0, EVEN)
         quantise_x(0, EVEN)
+        keep_busy(3)
 
         for cols in COLUMN_HALVES:
             cut = cols.start + VECTOR_COLS
             regroup(vector_copy, values_grouped, w_raw_values, slice(cols.start, cut))
             regroup(scalar_copy, values_grouped, w_raw_values, slice(cut, cols.stop))
-        quantise_x(0, ODD)
         for cols in COLUMN_HALVES:
             quantise_w(values_mx, values_grouped, cols)
+        transpose_x(0, ODD)
+        group_x(scalar_copy, 0, ODD)
+        quantise_x(0, ODD)
+        keep_busy(1)
 
         transpose_x(1, EVEN)
         transpose_x(1, ODD)
@@ -192,42 +206,26 @@ def tile_ammattention_pa_kernel(tc, x, w_kv, out_0, out_1, out_2):
         for copy, cols, acc in zip((scalar_copy, vector_copy), COLUMN_HALVES, halves):
             copy(out=v_sb[:, cols], in_=acc[:, cols])
         nc.sync.dma_start(out=v_view[:, 0, EVEN], in_=v_sb[:])
-        odd = multiply(0, (ODD,), values_mx)
-        sums = multiply(0, BOTH, values_mx)
-        transpose_x(2, EVEN)
         quantise_x(1, ODD)
-        store_value(vector_copy, 0, ODD, odd)
-        store_mean(scalar_halve, value_means, 0, sums)
+        store_value(0, ODD, multiply(0, (ODD,), values_mx))
+        store_mean(vector_halve, value_means, 0, multiply(0, BOTH, values_mx))
 
-        transpose_x(2, ODD)
-        even, sums, odd = multiply_values(1)
-        group_x(vector_copy, 2, EVEN)
-        transpose_x(3, EVEN)
-        regroup(vector_copy, keys_grouped, w_raw_keys, COLUMN_HALVES[0])
-        quantise_x(2, EVEN)
-        store_value(scalar_copy, 1, EVEN, even)
-        group_x(scalar_copy, 2, ODD)
-        transpose_x(3, ODD)
-        store_mean(vector_halve, value_means, 1, sums)
-        quantise_x(2, ODD)
-        store_value(scalar_copy, 1, ODD, odd)
-
-        even, sums, odd = multiply_values(2)
-        group_x(vector_copy, 3, EVEN)
-        group_x(scalar_copy, 3, ODD)
-        quantise_x(3, EVEN)
-        quantise_x(3, ODD)
-        regroup(vector_copy, keys_grouped, w_raw_keys, COLUMN_HALVES[1])
-        store_value(scalar_copy, 2, EVEN, even)
-        quantise_w(keys_mx, keys_grouped, slice(0, D))
-        store_mean(scalar_halve, value_means, 2, sums)
-        store_value(scalar_copy, 2, ODD, odd)
-
-        even, sums, odd = multiply_values(3)
-        store_value(vector_copy, 3, EVEN, even)
-        store_mean(scalar_halve, value_means, 3, sums)
-        store_value(scalar_copy, 3, ODD, odd)
+        for g in range(1, GROUPS):
+            even = multiply(g, (EVEN,), values_mx)
+            if g + 1 < GROUPS:
+                for s in BOTH:
+                    transpose_x(g + 1, s)
+            store_value(g, EVEN, even)
+            if g + 1 < GROUPS:
+                for s in BOTH:
+                    group_x(vector_copy, g + 1, s)
+                for s in BOTH:
+                    quantise_x(g + 1, s)
+            else:
+                quantise_w(keys_mx, keys_grouped, slice(0, D))
+            store_value(g, ODD, multiply(g, (ODD,), values_mx))
+            store_mean(vector_halve, value_means, g, multiply(g, BOTH, values_mx))
 
         for g in range(GROUPS):
-            halve = vector_halve if g % 2 == 0 else scalar_halve
+            halve = scalar_halve if g % 2 == 0 else vector_halve
             store_mean(halve, key_means, g, multiply(g, BOTH, keys_mx))

@@ -20,6 +20,7 @@ TOKENS = 1024
 D = 512
 SEG = 2
 GROUPS = TOKENS // (P * SEG)
+AHEAD = 2
 GPSIMD_COLS = 64
 RUN = 4
 KEYS, VALUES = 0, 1
@@ -116,6 +117,16 @@ def tile_ammattention_pa_kernel(tc, x, w_kv, out_0, out_1, out_2):
                 )
             return acc
 
+        def transpose_group(g):
+            for s in BOTH:
+                transpose_x(g, s)
+
+        def prepare_group(g):
+            for s in BOTH:
+                group_x(nc.vector.tensor_copy, g, s)
+            for s in BOTH:
+                quantise_x(g, s)
+
         def scalar_halve(out, acc):
             nc.scalar.activation(out=out, in_=acc[:], func=COPY, scale=1.0 / SEG)
 
@@ -147,12 +158,14 @@ def tile_ammattention_pa_kernel(tc, x, w_kv, out_0, out_1, out_2):
         identity = const.tile([P, P], F32)
         make_identity(nc, identity[:])
 
+        zeros = const.tile([P, P], F32)
+        nc.vector.memset(zeros[:], 0.0)
         unread = acc_psum.tile([P, P], F32, tag="acc")
 
         def keep_busy(matmuls):
             for i in range(matmuls):
                 nc.tensor.matmul(
-                    out=unread[:], lhsT=identity[:], rhs=identity[:], start=True, stop=True
+                    out=unread[:], lhsT=zeros[:], rhs=zeros[:], start=True, stop=True
                 )
 
         xts, x_grouped, x_mx = {}, {}, {}
@@ -167,7 +180,7 @@ def tile_ammattention_pa_kernel(tc, x, w_kv, out_0, out_1, out_2):
         values_grouped = w_pool.tile([P, D, PACK], BF16, align_bytes=64, name="w_grouped")
         keys_grouped = w_pool.tile([P, D, PACK], BF16, align_bytes=64, name="w_grouped")
 
-        for c in range(0, D, GPSIMD_COLS):
+        for c in range(0, D // 2, GPSIMD_COLS):
             cols = slice(c, c + GPSIMD_COLS)
             nc.gpsimd.tensor_scalar(
                 out=keys_grouped[:, cols, :],
@@ -182,7 +195,7 @@ def tile_ammattention_pa_kernel(tc, x, w_kv, out_0, out_1, out_2):
         transpose_x(0, EVEN)
         group_x(scalar_copy, 0, EVEN)
         quantise_x(0, EVEN)
-        keep_busy(3)
+        keep_busy(2)
 
         for cols in COLUMN_HALVES:
             cut = cols.start + VECTOR_COLS
@@ -207,24 +220,28 @@ def tile_ammattention_pa_kernel(tc, x, w_kv, out_0, out_1, out_2):
             copy(out=v_sb[:, cols], in_=acc[:, cols])
         nc.sync.dma_start(out=v_view[:, 0, EVEN], in_=v_sb[:])
         quantise_x(1, ODD)
-        store_value(0, ODD, multiply(0, (ODD,), values_mx))
-        store_mean(vector_halve, value_means, 0, multiply(0, BOTH, values_mx))
+        odd = multiply(0, (ODD,), values_mx)
+        transpose_group(2)
+        store_value(0, ODD, odd)
+        prepare_group(2)
 
         for g in range(1, GROUPS):
             even = multiply(g, (EVEN,), values_mx)
-            if g + 1 < GROUPS:
-                for s in BOTH:
-                    transpose_x(g + 1, s)
+            odd = multiply(g, (ODD,), values_mx)
+            sums = multiply(g - 1, BOTH, values_mx)
+            if g + AHEAD < GROUPS:
+                transpose_group(g + AHEAD)
             store_value(g, EVEN, even)
-            if g + 1 < GROUPS:
-                for s in BOTH:
-                    group_x(vector_copy, g + 1, s)
-                for s in BOTH:
-                    quantise_x(g + 1, s)
-            else:
+            store_value(g, ODD, odd)
+            if g + AHEAD == GROUPS:
+                regroup(vector_copy, keys_grouped, w_raw_keys, COLUMN_HALVES[1])
+                store_mean(scalar_halve, value_means, g - 1, sums)
                 quantise_w(keys_mx, keys_grouped, slice(0, D))
-            store_value(g, ODD, multiply(g, (ODD,), values_mx))
-            store_mean(vector_halve, value_means, g, multiply(g, BOTH, values_mx))
+            else:
+                store_mean(vector_halve, value_means, g - 1, sums)
+            if g + AHEAD < GROUPS:
+                prepare_group(g + AHEAD)
+        store_mean(vector_halve, value_means, GROUPS - 1, multiply(GROUPS - 1, BOTH, values_mx))
 
         for g in range(GROUPS):
             halve = scalar_halve if g % 2 == 0 else vector_halve

@@ -29,7 +29,7 @@ XT_BANKS = 3
 EVEN, ODD = 0, 1
 BOTH = (EVEN, ODD)
 COLUMN_HALVES = (slice(0, D // 2), slice(D // 2, D))
-VECTOR_COLS = 144
+VECTOR_COLS = 168
 
 FLOPS = 2 * TOKENS * D * (2 * D)
 

from contextlib import ExitStack

import concourse.mybir as mybir
from concourse.masks import make_identity

F32 = mybir.dt.float32
BF16 = mybir.dt.bfloat16
U32 = mybir.dt.uint32
U8 = mybir.dt.uint8
FP8X4 = mybir.dt.float8_e4m3fn_x4
COPY = mybir.ActivationFunctionType.Copy
MULT = mybir.AluOpType.mult
ADD = mybir.AluOpType.add

P = 128
PACK = 4
PAIR = 2
WORDS = PACK // PAIR
TOKENS = 1024
D = 512
SEG = 2
GROUPS = TOKENS // (P * SEG)
AHEAD = 2
GPSIMD_COLS = 64
RUN = 4
KEYS, VALUES = 0, 1
PSUM_BANKS = 8
XT_BANKS = 3
EVEN, ODD = 0, 1
BOTH = (EVEN, ODD)
COLUMN_HALVES = (slice(0, D // 2), slice(D // 2, D))
VECTOR_COLS = 168

FLOPS = 2 * TOKENS * D * (2 * D)


def tile_ammattention_pa_kernel(tc, x, w_kv, out_0, out_1, out_2):
    nc = tc.nc

    x_view = x.rearrange("b (p g s) k -> (b p) g s k", g=GROUPS, s=SEG)
    v_view = out_0.rearrange("b (p g s) d -> (b p) g s d", g=GROUPS, s=SEG)
    key_means = out_1.rearrange("b (p g) d -> (b p) g d", g=GROUPS)
    value_means = out_2.rearrange("b (p g) d -> (b p) g d", g=GROUPS)
    w_view = w_kv.rearrange("(q t) (h c) -> q h t c", t=PACK, h=2)

    with ExitStack() as ctx:
        const = ctx.enter_context(tc.tile_pool(name="const", bufs=1))
        w_pool = ctx.enter_context(tc.tile_pool(name="w", bufs=2))
        x_pool = ctx.enter_context(tc.tile_pool(name="x", bufs=GROUPS))
        x_mx_pool = ctx.enter_context(tc.tile_pool(name="x_mx", bufs=GROUPS * SEG))
        out_pool = ctx.enter_context(tc.tile_pool(name="out", bufs=GROUPS * SEG))
        xt_psum = ctx.enter_context(tc.psum_pool(name="xt", bufs=XT_BANKS))
        acc_psum = ctx.enter_context(tc.psum_pool(name="acc", bufs=PSUM_BANKS - XT_BANKS))
        ctx.enter_context(tc.manual_schedule())

        def load_w(half):
            w_raw = w_pool.tile([P, PACK, D], BF16)
            nc.sync.dma_start(out=w_raw[:], in_=w_view[:, half])
            return w_raw

        def load_x(g, tokens):
            nc.sync.dma_start(
                out=x_raws[g][:, tokens, :].rearrange("p s k -> p (s k)"),
                in_=x_view[:, g, tokens, :].rearrange("p s k -> p (s k)"),
            )

        def regroup(copy, w_grouped, w_raw, cols):
            copy(
                out=w_grouped[:, cols, :].rearrange("q (c i) t -> q c t i", i=RUN),
                in_=w_raw[:, :, cols].rearrange("q t (c i) -> q c t i", i=RUN),
            )

        def quantise_w(w_mx, w_grouped, cols):
            w_codes, w_scales = w_mx
            nc.vector.quantize_mx(
                out=w_codes[:, cols].bitcast(FP8X4),
                scales=w_scales[:, cols],
                in_=w_grouped[:, cols, :].rearrange("q c t -> q (c t)"),
            )

        def transpose_x(g, s):
            words = x_raws[g][:, s, :].bitcast(F32).rearrange("p (q u) -> p u q", u=WORDS)
            xt = xt_psum.tile([P, WORDS, P], F32)
            for u in range(WORDS):
                nc.tensor.transpose(xt[:, u, :], words[:, u, :], identity[:])
            xts[g, s] = xt

        def group_x(copy, g, s):
            grouped = x_mx_pool.tile([P, P * PACK], BF16, align_bytes=64)
            copy(
                out=grouped[:].bitcast(F32).rearrange("q (p u) -> q p u", u=WORDS),
                in_=xts[g, s][:].rearrange("q u p -> q p u"),
            )
            x_grouped[g, s] = grouped

        def quantise_x(g, s):
            x_codes = x_mx_pool.tile([P, P], U32, align_bytes=64)
            x_scales = x_mx_pool.tile([P, P], U8, align_bytes=64)
            nc.vector.quantize_mx(
                out=x_codes[:].bitcast(FP8X4), scales=x_scales[:], in_=x_grouped[g, s][:]
            )
            x_mx[g, s] = x_codes, x_scales

        def multiply(g, tokens, w_mx, cols=slice(0, D)):
            acc = acc_psum.tile([P, D], F32, tag="acc")
            w_codes, w_scales = w_mx
            for s in tokens:
                x_codes, x_scales = x_mx[g, s]
                nc.tensor.matmul_mx(
                    out=acc[:, cols],
                    lhsT=x_codes[:].bitcast(FP8X4),
                    lhsT_scale=x_scales[:],
                    rhs=w_codes[:, cols].bitcast(FP8X4),
                    rhs_scale=w_scales[:, cols],
                    start=(s == tokens[0]),
                    stop=(s == tokens[-1]),
                )
            return acc

        def transpose_group(g):
            for s in BOTH:
                transpose_x(g, s)

        def prepare_group(g):
            for s in BOTH:
                group_x(nc.vector.tensor_copy, g, s)
            for s in BOTH:
                quantise_x(g, s)

        def scalar_halve(out, acc):
            nc.scalar.activation(out=out, in_=acc[:], func=COPY, scale=1.0 / SEG)

        def vector_halve(out, acc):
            nc.vector.tensor_scalar_mul(out=out, in0=acc[:], scalar1=1.0 / SEG)

        def store_mean(halve, means, g, acc):
            mean = out_pool.tile([P, D], F32)
            halve(mean[:], acc)
            nc.sync.dma_start(out=means[:, g], in_=mean[:])

        def store_value(g, s, acc):
            v_sb = out_pool.tile([P, D], F32)
            nc.scalar.copy(out=v_sb[:], in_=acc[:])
            nc.sync.dma_start(out=v_view[:, g, s], in_=v_sb[:])

        x_raws = [x_pool.tile([P, SEG, D], BF16, name="x_raw") for g in range(GROUPS)]
        load_x(0, slice(EVEN, EVEN + 1))
        w_raw_values = load_w(VALUES)
        load_x(0, slice(ODD, ODD + 1))
        for g in range(1, GROUPS):
            load_x(g, slice(0, SEG))
        w_raw_keys = load_w(KEYS)

        warm = const.tile([P, 1], F32)
        nc.vector.memset(warm[:], 0.0)
        nc.scalar.activation(out=warm[:], in_=warm[:], func=COPY, scale=1.0 / SEG)

        identity = const.tile([P, P], F32)
        make_identity(nc, identity[:])

        zeros = const.tile([P, P], F32)
        nc.vector.memset(zeros[:], 0.0)
        unread = acc_psum.tile([P, P], F32, tag="acc")

        def keep_busy(matmuls):
            for i in range(matmuls):
                nc.tensor.matmul(
                    out=unread[:], lhsT=zeros[:], rhs=zeros[:], start=True, stop=True
                )

        xts, x_grouped, x_mx = {}, {}, {}
        scalar_copy, vector_copy = nc.scalar.copy, nc.vector.tensor_copy
        values_mx, keys_mx = [
            (
                w_pool.tile([P, D], U32, align_bytes=64, name="w_codes"),
                w_pool.tile([P, D], U8, align_bytes=64, name="w_scales"),
            )
            for half in range(2)
        ]
        values_grouped = w_pool.tile([P, D, PACK], BF16, align_bytes=64, name="w_grouped")
        keys_grouped = w_pool.tile([P, D, PACK], BF16, align_bytes=64, name="w_grouped")

        for c in range(0, D // 2, GPSIMD_COLS):
            cols = slice(c, c + GPSIMD_COLS)
            nc.gpsimd.tensor_scalar(
                out=keys_grouped[:, cols, :],
                in0=w_raw_keys[:, :, cols].rearrange("q t c -> q c t"),
                scalar1=1.0,
                scalar2=0.0,
                op0=MULT,
                op1=ADD,
            )

        keep_busy(3)
        transpose_x(0, EVEN)
        group_x(scalar_copy, 0, EVEN)
        quantise_x(0, EVEN)
        keep_busy(2)

        for cols in COLUMN_HALVES:
            cut = cols.start + VECTOR_COLS
            regroup(vector_copy, values_grouped, w_raw_values, slice(cols.start, cut))
            regroup(scalar_copy, values_grouped, w_raw_values, slice(cut, cols.stop))
        for cols in COLUMN_HALVES:
            quantise_w(values_mx, values_grouped, cols)
        transpose_x(0, ODD)
        group_x(scalar_copy, 0, ODD)
        quantise_x(0, ODD)
        keep_busy(1)

        transpose_x(1, EVEN)
        transpose_x(1, ODD)
        group_x(scalar_copy, 1, EVEN)
        group_x(vector_copy, 1, ODD)

        halves = [multiply(0, (EVEN,), values_mx, cols) for cols in COLUMN_HALVES]
        quantise_x(1, EVEN)
        v_sb = out_pool.tile([P, D], F32)
        for copy, cols, acc in zip((scalar_copy, vector_copy), COLUMN_HALVES, halves):
            copy(out=v_sb[:, cols], in_=acc[:, cols])
        nc.sync.dma_start(out=v_view[:, 0, EVEN], in_=v_sb[:])
        quantise_x(1, ODD)
        odd = multiply(0, (ODD,), values_mx)
        transpose_group(2)
        store_value(0, ODD, odd)
        prepare_group(2)

        for g in range(1, GROUPS):
            even = multiply(g, (EVEN,), values_mx)
            odd = multiply(g, (ODD,), values_mx)
            sums = multiply(g - 1, BOTH, values_mx)
            if g + AHEAD < GROUPS:
                transpose_group(g + AHEAD)
            store_value(g, EVEN, even)
            store_value(g, ODD, odd)
            if g + AHEAD == GROUPS:
                regroup(vector_copy, keys_grouped, w_raw_keys, COLUMN_HALVES[1])
                store_mean(scalar_halve, value_means, g - 1, sums)
                quantise_w(keys_mx, keys_grouped, slice(0, D))
            else:
                store_mean(vector_halve, value_means, g - 1, sums)
            if g + AHEAD < GROUPS:
                prepare_group(g + AHEAD)
        store_mean(vector_halve, value_means, GROUPS - 1, multiply(GROUPS - 1, BOTH, values_mx))

        for g in range(GROUPS):
            halve = scalar_halve if g % 2 == 0 else vector_halve
            store_mean(halve, key_means, g, multiply(g, BOTH, keys_mx))
